import numpy as np
import ml_dtypes


def mxq(x, axis, fmt="e4m3"):
    dtype, down = {"e4m3": (ml_dtypes.float8_e4m3fn, 7), "e5m2": (ml_dtypes.float8_e5m2, 14)}[fmt]
    v = np.moveaxis(np.asarray(x, np.float32).astype(ml_dtypes.bfloat16).astype(np.float64), axis, -1)
    blocks = v.reshape(v.shape[:-1] + (-1, 32))
    amax = np.abs(blocks).max(-1, keepdims=True)
    byte = np.maximum(np.where(amax > 0, np.frexp(amax)[1] - 1 + 127, 0) - down, 1)
    scale = np.exp2(byte - 127.0)
    codes = (blocks / scale).astype(np.float32).astype(dtype).astype(np.float64)
    return np.moveaxis((codes * scale).reshape(v.shape), -1, axis)


WIDE = False


def mx_kscale(k):
    if not WIDE:
        return np.ones(k)
    levels = np.array([10, -10, 5, -5, 0])
    if k % 512:
        return np.exp2(np.random.permutation(np.resize(levels, k // 32))).repeat(32)
    a = np.empty((k // 512, 16))
    for p in range(k // 512):
        a[p, :8] = np.random.permutation(np.resize(levels, 8))
        for g in range(8):
            far = levels[np.abs(levels - a[p, g]) >= 10]
            a[p, g + 8] = far[np.random.randint(len(far))]
    return np.exp2(a.ravel()).repeat(32)


BF16 = ml_dtypes.bfloat16


def bf(x):
    return np.asarray(x, np.float32).astype(BF16)


def f64(x):
    return np.asarray(x).astype(np.float64)


B, H, W, C, NF, ZD = 128, 4, 4, 8192, 128, 512
EPS = 1e-8
LRELU_SLOPE = 0.2


def setup_inputs():
    s = mx_kscale(C)
    return {"x": bf(np.random.standard_normal((B, H, W, C)) * s),
            "dlatents": bf(np.random.standard_normal((B, ZD))),
            "noise_map": bf(np.random.standard_normal((B, H, W, 1))),
            "conv_w": bf(np.random.standard_normal((C, NF)) / np.sqrt(C) / s[:, None]),
            "noise_weight": bf(np.random.standard_normal((1, 1, 1, NF)) * 0.5),
            "bias": bf(np.random.standard_normal((1, 1, 1, NF)) * 0.5),
            "dense_w": bf(np.random.standard_normal((ZD, 2 * NF)) / np.sqrt(ZD)),
            "dense_b": bf(np.random.standard_normal(2 * NF) * 0.3)}


def reference(x, dlatents, noise_map, conv_w, noise_weight, bias, dense_w, dense_b):
    y = mxq(f64(x), 3, "e4m3") @ mxq(f64(conv_w), 0, "e4m3")
    y = y + f64(noise_weight) * f64(noise_map) + f64(bias)
    y = np.where(y >= 0.0, y, LRELU_SLOPE * y)
    mu = np.mean(y, axis=(1, 2), keepdims=True)
    var = np.mean(np.square(y - mu), axis=(1, 2), keepdims=True)
    yn = (y - mu) / np.sqrt(var + EPS)
    gb = f64(dlatents) @ f64(dense_w) + f64(dense_b)
    nf = y.shape[-1]
    gb = gb.reshape(-1, 2, 1, 1, nf)
    gamma, beta = gb[:, 0], gb[:, 1]
    return yn * (1.0 + gamma) + beta

@@ -1,0 +1,342 @@
+from contextlib import ExitStack
+
+import concourse.mybir as mybir
+from concourse.masks import make_identity
+
+F32 = mybir.dt.float32
+BF16 = mybir.dt.bfloat16
+U32 = mybir.dt.uint32
+U8 = mybir.dt.uint8
+FP8X4 = mybir.dt.float8_e4m3fn_x4
+ALU = mybir.AluOpType
+ACT = mybir.ActivationFunctionType
+
+P = 128
+PIXELS = 16
+CHANNELS = 8192
+FILTERS = 128
+LATENT = 512
+EPS = 1e-8
+SLOPE = 0.2
+
+PACK = 4
+K_PASS = P * PACK
+PASSES = CHANNELS // K_PASS
+CHUNK_PASSES = 8
+CHUNK_COLS = CHUNK_PASSES * K_PASS
+CHUNKS_PER_PIXEL = PASSES // CHUNK_PASSES
+N_CHUNKS = PIXELS * CHUNKS_PER_PIXEL
+BANK_PASSES = 2
+BANKS_PER_CHUNK = CHUNK_PASSES // BANK_PASSES
+QUANT_PASSES = 8
+W_PIECES = 4
+W_PIECE_PASSES = PASSES // W_PIECES
+X_BUFS = 6
+
+FLOPS = 2 * P * PIXELS * CHANNELS * FILTERS + 2 * P * LATENT * 2 * FILTERS
+
+
+def tile_styleganlayerepilogue_k_kernel(
+    tc, x, dlatents, noise_map, conv_w, noise_weight, bias, dense_w, dense_b, out
+):
+    nc = tc.nc
+    x_rows = x.rearrange("b h w c -> b (h w) c")
+    out_rows = out.rearrange("b h w n -> b (h w) n")
+
+    with ExitStack() as ctx:
+        ctx.enter_context(tc.manual_schedule())
+        keep = ctx.enter_context(tc.tile_pool(name="keep", bufs=1))
+        x_pool = ctx.enter_context(tc.tile_pool(name="x_pool", bufs=X_BUFS))
+        grouped_pool = ctx.enter_context(tc.tile_pool(name="grouped_pool", bufs=3))
+        codes_pool = ctx.enter_context(tc.tile_pool(name="codes_pool", bufs=3))
+        work = ctx.enter_context(tc.tile_pool(name="work", bufs=3))
+        banks = ctx.enter_context(tc.psum_pool(name="banks", bufs=6))
+        sums = ctx.enter_context(tc.psum_pool(name="sums", bufs=2))
+
+        x_chunks = {}
+        grouped_tiles = {}
+        code_tiles = {}
+        scale_tiles = {}
+        conv_sums = {}
+        pre_relu = {}
+        squares = {}
+
+        latents = keep.tile([P, LATENT], BF16)
+        nc.scalar.dma_start(out=latents[:], in_=dlatents)
+        dense = keep.tile([P, LATENT // P, 2 * FILTERS], BF16)
+        nc.scalar.dma_start(out=dense[:], in_=dense_w.rearrange("(c p) n -> p c n", p=P))
+        noise_bf = keep.tile([P, PIXELS], BF16)
+        nc.scalar.dma_start(out=noise_bf[:], in_=noise_map.rearrange("b h w o -> b (h w o)"))
+        rows = keep.tile([P, 4 * FILTERS], BF16)
+        nc.vector.memset(rows[:], 0.0)
+        nc.scalar.dma_start(
+            out=rows[0:1, 0:FILTERS], in_=noise_weight.rearrange("a b c n -> (a b c) n")
+        )
+        nc.scalar.dma_start(
+            out=rows[0:1, FILTERS : 2 * FILTERS], in_=bias.rearrange("a b c n -> (a b c) n")
+        )
+        nc.scalar.dma_start(
+            out=rows[0:1, 2 * FILTERS : 4 * FILTERS], in_=dense_b.rearrange("(o n) -> o n", o=1)
+        )
+
+        w_raw = keep.tile([P, PASSES, PACK, FILTERS], BF16)
+        w_view = conv_w.rearrange("(c p t) n -> p c (t n)", p=P, t=PACK)
+        for piece in range(W_PIECES):
+            passes = slice(piece * W_PIECE_PASSES, (piece + 1) * W_PIECE_PASSES)
+            nc.sync.dma_start(
+                out=w_raw[:, passes, :, :].rearrange("p c t n -> p c (t n)"),
+                in_=w_view[:, passes, :],
+            )
+
+        def load(i):
+            if i >= N_CHUNKS:
+                return
+            pixel, part = divmod(i, CHUNKS_PER_PIXEL)
+            x_chunk = x_pool.tile([P, CHUNK_COLS], BF16, name="x_chunk")
+            nc.sync.dma_start(
+                out=x_chunk[:], in_=x_rows[:, pixel, part * CHUNK_COLS : (part + 1) * CHUNK_COLS]
+            )
+            x_chunks[i] = x_chunk
+
+        for i in range(X_BUFS):
+            load(i)
+
+        ident_f32 = keep.tile([P, P], F32)
+        make_identity(nc, ident_f32[:])
+        ident_bf = keep.tile([P, P], BF16)
+        make_identity(nc, ident_bf[:])
+        ones = keep.tile([P, P], BF16)
+        nc.vector.memset(ones[:], 1.0)
+        dev_sum = keep.tile([P, FILTERS], F32)
+        nc.vector.memset(dev_sum[:], 0.0)
+        sq_sum = keep.tile([P, FILTERS], F32)
+        nc.vector.memset(sq_sum[:], 0.0)
+        one = keep.tile([P, 1], F32)
+        nc.vector.memset(one[:], 1.0)
+        warm = keep.tile([P, 1], F32)
+        nc.scalar.activation(out=warm[:], in_=one[:], func=ACT.Sqrt)
+
+        latents_t_ps = banks.tile([P, LATENT // P, P], BF16, tag="bank")
+        for c in range(LATENT // P):
+            nc.tensor.transpose(latents_t_ps[:, c, :], latents[:, c * P : (c + 1) * P], ident_bf[:])
+        latents_t = keep.tile([P, LATENT // P, P], BF16)
+        nc.vector.tensor_copy(out=latents_t[:], in_=latents_t_ps[:])
+
+        spread_ps = banks.tile([P, 4 * FILTERS], F32, tag="bank")
+        nc.tensor.matmul(
+            out=spread_ps[:, 0 : 2 * FILTERS],
+            lhsT=ones[:],
+            rhs=rows[:, 0 : 2 * FILTERS],
+            start=True,
+            stop=True,
+        )
+        for c in range(LATENT // P):
+            nc.tensor.matmul(
+                out=spread_ps[:, 2 * FILTERS : 4 * FILTERS],
+                lhsT=latents_t[:, c, :],
+                rhs=dense[:, c, :],
+                start=(c == 0),
+                stop=False,
+            )
+        nc.tensor.matmul(
+            out=spread_ps[:, 2 * FILTERS : 4 * FILTERS],
+            lhsT=ones[:],
+            rhs=rows[:, 2 * FILTERS : 4 * FILTERS],
+            start=False,
+            stop=True,
+        )
+        per_channel = keep.tile([P, 2 * FILTERS], F32)
+        nc.vector.tensor_copy(out=per_channel[:], in_=spread_ps[:, 0 : 2 * FILTERS])
+        gamma1 = keep.tile([P, FILTERS], F32)
+        nc.vector.tensor_scalar_add(
+            out=gamma1[:], in0=spread_ps[:, 2 * FILTERS : 3 * FILTERS], scalar1=1.0
+        )
+        beta = keep.tile([P, FILTERS], F32)
+        nc.vector.tensor_copy(out=beta[:], in_=spread_ps[:, 3 * FILTERS : 4 * FILTERS])
+
+        noise = keep.tile([P, PIXELS], F32)
+        nc.vector.tensor_copy(out=noise[:], in_=noise_bf[:])
+        noise_bias = keep.tile([P, PIXELS, FILTERS], F32)
+        for pixel in range(PIXELS):
+            nc.vector.scalar_tensor_tensor(
+                out=noise_bias[:, pixel, :],
+                in0=per_channel[:, 0:FILTERS],
+                scalar=noise[:, pixel : pixel + 1],
+                in1=per_channel[:, FILTERS : 2 * FILTERS],
+                op0=ALU.mult,
+                op1=ALU.add,
+            )
+
+        w_grouped = keep.tile([P, PASSES, FILTERS, PACK], BF16, align_bytes=64)
+        w_codes = keep.tile([P, PASSES * FILTERS], U32, align_bytes=64)
+        w_scales = keep.tile([P, PASSES * FILTERS], U8, align_bytes=64)
+        for piece in range(W_PIECES):
+            passes = slice(piece * W_PIECE_PASSES, (piece + 1) * W_PIECE_PASSES)
+            regroup = nc.scalar.copy if piece % 2 == 0 else nc.vector.tensor_copy
+            regroup(
+                out=w_grouped[:, passes, :, :],
+                in_=w_raw[:, passes, :, :].rearrange("p c t n -> p c n t"),
+            )
+        for piece in range(W_PIECES):
+            passes = slice(piece * W_PIECE_PASSES, (piece + 1) * W_PIECE_PASSES)
+            cols = slice(piece * W_PIECE_PASSES * FILTERS, (piece + 1) * W_PIECE_PASSES * FILTERS)
+            nc.vector.quantize_mx(
+                out=w_codes[:, cols].bitcast(FP8X4),
+                scales=w_scales[:, cols],
+                in_=w_grouped[:, passes, :, :].rearrange("p c n t -> p (c n t)"),
+            )
+
+        def transpose(i):
+            if i >= N_CHUNKS:
+                return
+            words = x_chunks[i][:].bitcast(F32)
+            grouped = grouped_pool.tile([P, CHUNK_COLS], BF16, align_bytes=64, name="grouped")
+            grouped_words = grouped[:].bitcast(F32).rearrange("p (g r u) -> p g r u", r=P, u=2)
+            for bank in range(BANKS_PER_CHUNK):
+                xt = banks.tile([P, BANK_PASSES, 2, P], F32, tag="bank", name="xt")
+                for g in range(BANK_PASSES):
+                    for u in range(2):
+                        first = (bank * BANK_PASSES + g) * 2 * P
+                        nc.tensor.transpose(
+                            xt[:, g, u, :], words[:, first + u : first + 2 * P : 2], ident_f32[:]
+                        )
+                empty = nc.vector.tensor_copy if bank == BANKS_PER_CHUNK - 1 else nc.scalar.copy
+                empty(
+                    out=grouped_words[:, bank * BANK_PASSES : (bank + 1) * BANK_PASSES, :, :],
+                    in_=xt[:].rearrange("p g u r -> p g r u"),
+                )
+            grouped_tiles[i] = grouped
+
+        def quantise(i):
+            if i < 0 or i >= N_CHUNKS:
+                return
+            codes = codes_pool.tile([P, CHUNK_PASSES * P], U32, align_bytes=64, name="codes")
+            scales = codes_pool.tile([P, CHUNK_PASSES * P], U8, align_bytes=64, name="scales")
+            for first in range(0, CHUNK_PASSES, QUANT_PASSES):
+                cols = slice(first * P, (first + QUANT_PASSES) * P)
+                values = slice(first * P * PACK, (first + QUANT_PASSES) * P * PACK)
+                nc.vector.quantize_mx(
+                    out=codes[:, cols].bitcast(FP8X4),
+                    scales=scales[:, cols],
+                    in_=grouped_tiles[i][:, values],
+                )
+            code_tiles[i] = codes
+            scale_tiles[i] = scales
+
+        def multiply(i):
+            if i < 0 or i >= N_CHUNKS:
+                return
+            pixel, part = divmod(i, CHUNKS_PER_PIXEL)
+            if part == 0:
+                conv_sums[pixel] = sums.tile([P, FILTERS], F32, name="conv_sum")
+            for g in range(CHUNK_PASSES):
+                c = part * CHUNK_PASSES + g
+                nc.tensor.matmul_mx(
+                    out=conv_sums[pixel][:],
+                    lhsT=code_tiles[i][:, g * P : (g + 1) * P].bitcast(FP8X4),
+                    lhsT_scale=scale_tiles[i][:, g * P : (g + 1) * P],
+                    rhs=w_codes[:, c * FILTERS : (c + 1) * FILTERS].bitcast(FP8X4),
+                    rhs_scale=w_scales[:, c * FILTERS : (c + 1) * FILTERS],
+                    start=(c == 0),
+                    stop=(c == PASSES - 1),
+                )
+
+        def closes_pixel(i):
+            return 0 <= i < N_CHUNKS and i % CHUNKS_PER_PIXEL == CHUNKS_PER_PIXEL - 1
+
+        relu = keep.tile([P, PIXELS, FILTERS], F32)
+        dev = keep.tile([P, PIXELS, FILTERS], F32)
+
+        def add_noise(i):
+            if not closes_pixel(i):
+                return
+            pixel = i // CHUNKS_PER_PIXEL
+            pre_relu[pixel] = work.tile([P, FILTERS], F32, name="pre")
+            nc.vector.tensor_tensor(
+                out=pre_relu[pixel][:],
+                in0=conv_sums[pixel][:],
+                in1=noise_bias[:, pixel, :],
+                op=ALU.add,
+            )
+
+        def leaky_relu(i):
+            if not closes_pixel(i):
+                return
+            pixel = i // CHUNKS_PER_PIXEL
+            nc.vector.scalar_tensor_tensor(
+                out=relu[:, pixel, :],
+                in0=pre_relu[pixel][:],
+                scalar=SLOPE,
+                in1=pre_relu[pixel][:],
+                op0=ALU.mult,
+                op1=ALU.max,
+            )
+            nc.gpsimd.tensor_tensor(
+                out=dev[:, pixel, :], in0=relu[:, pixel, :], in1=relu[:, 0, :], op=ALU.subtract
+            )
+            nc.gpsimd.tensor_tensor(
+                out=dev_sum[:], in0=dev_sum[:], in1=dev[:, pixel, :], op=ALU.add
+            )
+
+        def square(i):
+            if not closes_pixel(i):
+                return
+            pixel = i // CHUNKS_PER_PIXEL
+            squares[pixel] = work.tile([P, FILTERS], F32, name="sq")
+            nc.scalar.activation(out=squares[pixel][:], in_=dev[:, pixel, :], func=ACT.Square)
+            nc.gpsimd.tensor_tensor(out=sq_sum[:], in0=sq_sum[:], in1=squares[pixel][:], op=ALU.add)
+
+        for step in range(N_CHUNKS + 3):
+            add_noise(step - 3)
+            quantise(step - 1)
+            leaky_relu(step - 3)
+            transpose(step)
+            load(step + X_BUFS)
+            multiply(step - 2)
+            square(step - 3)
+
+        mean = keep.tile([P, FILTERS], F32)
+        nc.vector.tensor_scalar_mul(out=mean[:], in0=dev_sum[:], scalar1=1.0 / PIXELS)
+        mean_sq = keep.tile([P, FILTERS], F32)
+        nc.vector.tensor_mul(out=mean_sq[:], in0=mean[:], in1=mean[:])
+        second = keep.tile([P, FILTERS], F32)
+        nc.vector.tensor_scalar(
+            out=second[:],
+            in0=sq_sum[:],
+            scalar1=1.0 / PIXELS,
+            scalar2=EPS,
+            op0=ALU.mult,
+            op1=ALU.add,
+        )
+        var_eps = keep.tile([P, FILTERS], F32)
+        nc.vector.tensor_sub(out=var_eps[:], in0=second[:], in1=mean_sq[:])
+        std = keep.tile([P, FILTERS], F32)
+        nc.scalar.activation(out=std[:], in_=var_eps[:], func=ACT.Sqrt)
+        inv_std = keep.tile([P, FILTERS], F32)
+        nc.vector.reciprocal(out=inv_std[:], in_=std[:])
+        gain = keep.tile([P, FILTERS], F32)
+        nc.vector.tensor_mul(out=gain[:], in0=inv_std[:], in1=gamma1[:])
+        mean_gain = keep.tile([P, FILTERS], F32)
+        nc.vector.tensor_mul(out=mean_gain[:], in0=mean[:], in1=gain[:])
+        shift = keep.tile([P, FILTERS], F32)
+        nc.vector.tensor_sub(out=shift[:], in0=beta[:], in1=mean_gain[:])
+
+        result = keep.tile([P, PIXELS, FILTERS], F32)
+        STORE_PIXELS = 4
+        for first in range(0, PIXELS, STORE_PIXELS):
+            some = slice(first, first + STORE_PIXELS)
+            nc.vector.tensor_tensor(
+                out=result[:, some, :],
+                in0=dev[:, some, :],
+                in1=gain[:].unsqueeze(1).to_broadcast([P, STORE_PIXELS, FILTERS]),
+                op=ALU.mult,
+            )
+        for first in range(0, PIXELS, STORE_PIXELS):
+            some = slice(first, first + STORE_PIXELS)
+            nc.vector.tensor_tensor(
+                out=result[:, some, :],
+                in0=result[:, some, :],
+                in1=shift[:].unsqueeze(1).to_broadcast([P, STORE_PIXELS, FILTERS]),
+                op=ALU.add,
+            )
+            nc.sync.dma_start(out=out_rows[:, some, :], in_=result[:, some, :])

@@ -10,9 +10,12 @@ U8 = mybir.dt.uint8
 FP8X4 = mybir.dt.float8_e4m3fn_x4
 ALU = mybir.AluOpType
 ACT = mybir.ActivationFunctionType
+AXIS = mybir.AxisListType
 
 P = 128
+SAMPLES = 128
 PIXELS = 16
+ROWS = SAMPLES * PIXELS
 CHANNELS = 8192
 FILTERS = 128
 LATENT = 512
@@ -22,321 +25,416 @@ SLOPE = 0.2
 PACK = 4
 K_PASS = P * PACK
 PASSES = CHANNELS // K_PASS
-CHUNK_PASSES = 8
+TILES = 2
+GROUP_ROWS = TILES * P
+GROUP_SAMPLES = GROUP_ROWS // PIXELS
+GROUPS = ROWS // GROUP_ROWS
+CHUNK_PASSES = 4
 CHUNK_COLS = CHUNK_PASSES * K_PASS
-CHUNKS_PER_PIXEL = PASSES // CHUNK_PASSES
-N_CHUNKS = PIXELS * CHUNKS_PER_PIXEL
-BANK_PASSES = 2
-BANKS_PER_CHUNK = CHUNK_PASSES // BANK_PASSES
-QUANT_PASSES = 8
-W_PIECES = 4
-W_PIECE_PASSES = PASSES // W_PIECES
-X_BUFS = 6
+CHUNKS = PASSES // CHUNK_PASSES
+STEPS = GROUPS * CHUNKS
+X_BUFS = 10
+SORTED = (1, 3)
 
-FLOPS = 2 * P * PIXELS * CHANNELS * FILTERS + 2 * P * LATENT * 2 * FILTERS
+FLOPS = 2 * ROWS * CHANNELS * FILTERS + 2 * SAMPLES * LATENT * 2 * FILTERS
 
 
 def tile_styleganlayerepilogue_k_kernel(
     tc, x, dlatents, noise_map, conv_w, noise_weight, bias, dense_w, dense_b, out
 ):
     nc = tc.nc
-    x_rows = x.rearrange("b h w c -> b (h w) c")
-    out_rows = out.rearrange("b h w n -> b (h w) n")
+    x_rows = x.rearrange("b h w c -> (b h w) c").rearrange("(g s p) c -> g p s c", s=TILES, p=P)
+    out_rows = out.rearrange("b h w n -> (b h w) n").rearrange("(g s p) n -> g p s n", s=TILES, p=P)
 
     with ExitStack() as ctx:
         ctx.enter_context(tc.manual_schedule())
         keep = ctx.enter_context(tc.tile_pool(name="keep", bufs=1))
         x_pool = ctx.enter_context(tc.tile_pool(name="x_pool", bufs=X_BUFS))
+        sorted_pool = ctx.enter_context(tc.tile_pool(name="sorted_pool", bufs=3))
         grouped_pool = ctx.enter_context(tc.tile_pool(name="grouped_pool", bufs=3))
         codes_pool = ctx.enter_context(tc.tile_pool(name="codes_pool", bufs=3))
-        work = ctx.enter_context(tc.tile_pool(name="work", bufs=3))
+        work = ctx.enter_context(tc.tile_pool(name="work", bufs=2))
         banks = ctx.enter_context(tc.psum_pool(name="banks", bufs=6))
         sums = ctx.enter_context(tc.psum_pool(name="sums", bufs=2))
 
         x_chunks = {}
+        sorted_words = {}
         grouped_tiles = {}
         code_tiles = {}
         scale_tiles = {}
         conv_sums = {}
-        pre_relu = {}
-        squares = {}
+        epilogue = {}
 
-        latents = keep.tile([P, LATENT], BF16)
-        nc.scalar.dma_start(out=latents[:], in_=dlatents)
-        dense = keep.tile([P, LATENT // P, 2 * FILTERS], BF16)
-        nc.scalar.dma_start(out=dense[:], in_=dense_w.rearrange("(c p) n -> p c n", p=P))
-        noise_bf = keep.tile([P, PIXELS], BF16)
-        nc.scalar.dma_start(out=noise_bf[:], in_=noise_map.rearrange("b h w o -> b (h w o)"))
-        rows = keep.tile([P, 4 * FILTERS], BF16)
-        nc.vector.memset(rows[:], 0.0)
-        nc.scalar.dma_start(
-            out=rows[0:1, 0:FILTERS], in_=noise_weight.rearrange("a b c n -> (a b c) n")
-        )
-        nc.scalar.dma_start(
-            out=rows[0:1, FILTERS : 2 * FILTERS], in_=bias.rearrange("a b c n -> (a b c) n")
-        )
-        nc.scalar.dma_start(
-            out=rows[0:1, 2 * FILTERS : 4 * FILTERS], in_=dense_b.rearrange("(o n) -> o n", o=1)
-        )
+        def load(i):
+            if i >= STEPS:
+                return
+            group, part = divmod(i, CHUNKS)
+            x_chunk = x_pool.tile([P, TILES, CHUNK_COLS], BF16, name="x_chunk")
+            cols = slice(part * CHUNK_COLS, (part + 1) * CHUNK_COLS)
+            if i == 0:
+                for s in range(TILES):
+                    nc.sync.dma_start(out=x_chunk[:, s, :], in_=x_rows[group, :, s, cols])
+            else:
+                nc.sync.dma_start(out=x_chunk[:], in_=x_rows[group, :, :, cols])
+            x_chunks[i] = x_chunk
 
         w_raw = keep.tile([P, PASSES, PACK, FILTERS], BF16)
         w_view = conv_w.rearrange("(c p t) n -> p c (t n)", p=P, t=PACK)
-        for piece in range(W_PIECES):
-            passes = slice(piece * W_PIECE_PASSES, (piece + 1) * W_PIECE_PASSES)
+
+        def load_w(part):
+            passes = slice(part * CHUNK_PASSES, (part + 1) * CHUNK_PASSES)
             nc.sync.dma_start(
                 out=w_raw[:, passes, :, :].rearrange("p c t n -> p c (t n)"),
                 in_=w_view[:, passes, :],
             )
 
-        def load(i):
-            if i >= N_CHUNKS:
-                return
-            pixel, part = divmod(i, CHUNKS_PER_PIXEL)
-            x_chunk = x_pool.tile([P, CHUNK_COLS], BF16, name="x_chunk")
+        vectors = keep.tile([P, FILTERS], BF16)
+        nc.vector.memset(vectors[:], 0.0)
+        noise_rows = keep.tile([P, ROWS], BF16)
+        nc.vector.memset(noise_rows[:], 1.0)
+        dense_rows = keep.tile([P, 2 * FILTERS], BF16)
+        nc.vector.memset(dense_rows[:], 0.0)
+        latents = keep.tile([P, LATENT], BF16)
+        dense = keep.tile([P, LATENT // P, 2 * FILTERS], BF16)
+
+        def load_noise():
             nc.sync.dma_start(
-                out=x_chunk[:], in_=x_rows[:, pixel, part * CHUNK_COLS : (part + 1) * CHUNK_COLS]
+                out=noise_rows[0:1, :], in_=noise_map.rearrange("b h w o -> o (b h w)")
             )
-            x_chunks[i] = x_chunk
+            nc.sync.dma_start(
+                out=vectors[0:1, :], in_=noise_weight.rearrange("a b c n -> (a b c) n")
+            )
+            nc.sync.dma_start(out=vectors[1:2, :], in_=bias.rearrange("a b c n -> (a b c) n"))
+
+        def load_style():
+            nc.sync.dma_start(out=latents[:], in_=dlatents)
+            nc.sync.dma_start(out=dense[:], in_=dense_w.rearrange("(c p) n -> p c n", p=P))
+            nc.sync.dma_start(out=dense_rows[0:1, :], in_=dense_b.rearrange("(o n) -> o n", o=1))
 
         for i in range(X_BUFS):
             load(i)
+            if i == 1:
+                load_noise()
+            if i == 3:
+                load_style()
+            if i < CHUNKS:
+                load_w(i)
 
         ident_f32 = keep.tile([P, P], F32)
         make_identity(nc, ident_f32[:])
-        ident_bf = keep.tile([P, P], BF16)
-        make_identity(nc, ident_bf[:])
-        ones = keep.tile([P, P], BF16)
-        nc.vector.memset(ones[:], 1.0)
-        dev_sum = keep.tile([P, FILTERS], F32)
-        nc.vector.memset(dev_sum[:], 0.0)
-        sq_sum = keep.tile([P, FILTERS], F32)
-        nc.vector.memset(sq_sum[:], 0.0)
         one = keep.tile([P, 1], F32)
         nc.vector.memset(one[:], 1.0)
         warm = keep.tile([P, 1], F32)
-        nc.scalar.activation(out=warm[:], in_=one[:], func=ACT.Sqrt)
+        nc.scalar.activation(out=warm[:], in_=one[:], func=ACT.Abs_reciprocal_sqrt)
+        ident_bf = keep.tile([P, P], BF16)
+        make_identity(nc, ident_bf[:])
 
-        latents_t_ps = banks.tile([P, LATENT // P, P], BF16, tag="bank")
-        for c in range(LATENT // P):
-            nc.tensor.transpose(latents_t_ps[:, c, :], latents[:, c * P : (c + 1) * P], ident_bf[:])
-        latents_t = keep.tile([P, LATENT // P, P], BF16)
-        nc.vector.tensor_copy(out=latents_t[:], in_=latents_t_ps[:])
+        ones = keep.tile([P, SAMPLES], BF16)
+        nc.vector.memset(ones[:], 1.0)
 
-        spread_ps = banks.tile([P, 4 * FILTERS], F32, tag="bank")
-        nc.tensor.matmul(
-            out=spread_ps[:, 0 : 2 * FILTERS],
-            lhsT=ones[:],
-            rhs=rows[:, 0 : 2 * FILTERS],
-            start=True,
-            stop=True,
-        )
-        for c in range(LATENT // P):
+        noise_bias = keep.tile([P, ROWS], F32)
+        latents_t = keep.tile([P, LATENT // P, SAMPLES], BF16)
+        gamma1 = keep.tile([P, SAMPLES], F32)
+        beta = keep.tile([P, SAMPLES], F32)
+
+        def noise_table(first):
+            cols = slice(first, first + 512)
+            noise_ps = banks.tile([P, 512], F32, tag="bank", name="noise_ps")
             nc.tensor.matmul(
-                out=spread_ps[:, 2 * FILTERS : 4 * FILTERS],
-                lhsT=latents_t[:, c, :],
-                rhs=dense[:, c, :],
-                start=(c == 0),
-                stop=False,
+                out=noise_ps[:], lhsT=vectors[:], rhs=noise_rows[:, cols], start=True, stop=True
             )
-        nc.tensor.matmul(
-            out=spread_ps[:, 2 * FILTERS : 4 * FILTERS],
-            lhsT=ones[:],
-            rhs=rows[:, 2 * FILTERS : 4 * FILTERS],
-            start=False,
-            stop=True,
-        )
-        per_channel = keep.tile([P, 2 * FILTERS], F32)
-        nc.vector.tensor_copy(out=per_channel[:], in_=spread_ps[:, 0 : 2 * FILTERS])
-        gamma1 = keep.tile([P, FILTERS], F32)
-        nc.vector.tensor_scalar_add(
-            out=gamma1[:], in0=spread_ps[:, 2 * FILTERS : 3 * FILTERS], scalar1=1.0
-        )
-        beta = keep.tile([P, FILTERS], F32)
-        nc.vector.tensor_copy(out=beta[:], in_=spread_ps[:, 3 * FILTERS : 4 * FILTERS])
+            nc.scalar.copy(out=noise_bias[:, cols], in_=noise_ps[:])
 
-        noise = keep.tile([P, PIXELS], F32)
-        nc.vector.tensor_copy(out=noise[:], in_=noise_bf[:])
-        noise_bias = keep.tile([P, PIXELS, FILTERS], F32)
-        for pixel in range(PIXELS):
-            nc.vector.scalar_tensor_tensor(
-                out=noise_bias[:, pixel, :],
-                in0=per_channel[:, 0:FILTERS],
-                scalar=noise[:, pixel : pixel + 1],
-                in1=per_channel[:, FILTERS : 2 * FILTERS],
-                op0=ALU.mult,
-                op1=ALU.add,
-            )
+        def turn_latents():
+            latents_ps = banks.tile([P, LATENT // P, SAMPLES], BF16, tag="bank", name="latents_ps")
+            for c in range(LATENT // P):
+                nc.tensor.transpose(
+                    latents_ps[:, c, :], latents[:, c * P : (c + 1) * P], ident_bf[:]
+                )
+            nc.vector.tensor_copy(out=latents_t[:], in_=latents_ps[:])
+
+        def style_table():
+            style_ps = banks.tile([P, 2, SAMPLES], F32, tag="bank", name="style_ps")
+            for half in range(2):
+                cols = slice(half * FILTERS, (half + 1) * FILTERS)
+                for c in range(LATENT // P):
+                    nc.tensor.matmul(
+                        out=style_ps[:, half, :],
+                        lhsT=dense[:, c, cols],
+                        rhs=latents_t[:, c, :],
+                        start=(c == 0),
+                        stop=False,
+                    )
+                nc.tensor.matmul(
+                    out=style_ps[:, half, :],
+                    lhsT=dense_rows[:, cols],
+                    rhs=ones[:],
+                    start=False,
+                    stop=True,
+                )
+            nc.vector.tensor_scalar_add(out=gamma1[:], in0=style_ps[:, 0, :], scalar1=1.0)
+            nc.vector.tensor_copy(out=beta[:], in_=style_ps[:, 1, :])
 
         w_grouped = keep.tile([P, PASSES, FILTERS, PACK], BF16, align_bytes=64)
         w_codes = keep.tile([P, PASSES * FILTERS], U32, align_bytes=64)
         w_scales = keep.tile([P, PASSES * FILTERS], U8, align_bytes=64)
-        for piece in range(W_PIECES):
-            passes = slice(piece * W_PIECE_PASSES, (piece + 1) * W_PIECE_PASSES)
-            regroup = nc.scalar.copy if piece % 2 == 0 else nc.vector.tensor_copy
-            regroup(
+
+        def group_w(part):
+            passes = slice(part * CHUNK_PASSES, (part + 1) * CHUNK_PASSES)
+            nc.vector.tensor_copy(
                 out=w_grouped[:, passes, :, :],
                 in_=w_raw[:, passes, :, :].rearrange("p c t n -> p c n t"),
             )
-        for piece in range(W_PIECES):
-            passes = slice(piece * W_PIECE_PASSES, (piece + 1) * W_PIECE_PASSES)
-            cols = slice(piece * W_PIECE_PASSES * FILTERS, (piece + 1) * W_PIECE_PASSES * FILTERS)
+
+        def quantise_w(part):
+            passes = slice(part * CHUNK_PASSES, (part + 1) * CHUNK_PASSES)
+            cols = slice(part * CHUNK_PASSES * FILTERS, (part + 1) * CHUNK_PASSES * FILTERS)
             nc.vector.quantize_mx(
                 out=w_codes[:, cols].bitcast(FP8X4),
                 scales=w_scales[:, cols],
                 in_=w_grouped[:, passes, :, :].rearrange("p c n t -> p (c n t)"),
             )
 
-        def transpose(i):
-            if i >= N_CHUNKS:
+        def sorted_passes(i):
+            return SORTED if i >= CHUNKS else ()
+
+        def sort_words(i, which):
+            if i >= STEPS or which >= len(sorted_passes(i)):
                 return
+            g = sorted_passes(i)[which]
+            tile = sorted_pool.tile([P, TILES, 2, P], F32, tag="sorted%d" % which, name="in_order")
+            words = x_chunks[i][:, :, g * K_PASS : (g + 1) * K_PASS].bitcast(F32)
+            nc.vector.tensor_copy(out=tile[:], in_=words.rearrange("p s (r u) -> p s u r", u=2))
+            sorted_words[i, g] = tile
+
+        def transpose(i):
             words = x_chunks[i][:].bitcast(F32)
-            grouped = grouped_pool.tile([P, CHUNK_COLS], BF16, align_bytes=64, name="grouped")
-            grouped_words = grouped[:].bitcast(F32).rearrange("p (g r u) -> p g r u", r=P, u=2)
-            for bank in range(BANKS_PER_CHUNK):
-                xt = banks.tile([P, BANK_PASSES, 2, P], F32, tag="bank", name="xt")
-                for g in range(BANK_PASSES):
+            grouped = grouped_pool.tile(
+                [P, CHUNK_PASSES, GROUP_ROWS * PACK], BF16, align_bytes=64, name="grouped"
+            )
+            for g in range(CHUNK_PASSES):
+                xt = banks.tile([P, TILES, 2, P], F32, tag="bank", name="xt")
+                for s in range(TILES):
                     for u in range(2):
-                        first = (bank * BANK_PASSES + g) * 2 * P
-                        nc.tensor.transpose(
-                            xt[:, g, u, :], words[:, first + u : first + 2 * P : 2], ident_f32[:]
-                        )
-                empty = nc.vector.tensor_copy if bank == BANKS_PER_CHUNK - 1 else nc.scalar.copy
-                empty(
-                    out=grouped_words[:, bank * BANK_PASSES : (bank + 1) * BANK_PASSES, :, :],
-                    in_=xt[:].rearrange("p g u r -> p g r u"),
+                        if (i, g) in sorted_words:
+                            source = sorted_words[i, g][:, s, u, :]
+                        else:
+                            source = words[:, s, g * 2 * P + u : (g + 1) * 2 * P : 2]
+                        nc.tensor.transpose(xt[:, s, u, :], source, ident_f32[:])
+                nc.scalar.copy(
+                    out=grouped[:, g, :].bitcast(F32).rearrange("p (s r u) -> p s r u", s=TILES, u=2),
+                    in_=xt[:].rearrange("p s u r -> p s r u"),
                 )
+                scalar_epilogue(i, g)
+                if g == 1:
+                    vector_epilogue(i, 2)
+                    sort_words(i + 1, 1)
             grouped_tiles[i] = grouped
 
         def quantise(i):
-            if i < 0 or i >= N_CHUNKS:
+            if i < 0 or i >= STEPS:
                 return
-            codes = codes_pool.tile([P, CHUNK_PASSES * P], U32, align_bytes=64, name="codes")
-            scales = codes_pool.tile([P, CHUNK_PASSES * P], U8, align_bytes=64, name="scales")
-            for first in range(0, CHUNK_PASSES, QUANT_PASSES):
-                cols = slice(first * P, (first + QUANT_PASSES) * P)
-                values = slice(first * P * PACK, (first + QUANT_PASSES) * P * PACK)
-                nc.vector.quantize_mx(
-                    out=codes[:, cols].bitcast(FP8X4),
-                    scales=scales[:, cols],
-                    in_=grouped_tiles[i][:, values],
-                )
+            codes = codes_pool.tile([P, CHUNK_PASSES * GROUP_ROWS], U32, align_bytes=64, name="codes")
+            scales = codes_pool.tile([P, CHUNK_PASSES * GROUP_ROWS], U8, align_bytes=64, name="scales")
+            nc.vector.quantize_mx(
+                out=codes[:].bitcast(FP8X4),
+                scales=scales[:],
+                in_=grouped_tiles[i][:].rearrange("p c r -> p (c r)"),
+            )
             code_tiles[i] = codes
             scale_tiles[i] = scales
 
         def multiply(i):
-            if i < 0 or i >= N_CHUNKS:
+            if i < 0 or i >= STEPS:
                 return
-            pixel, part = divmod(i, CHUNKS_PER_PIXEL)
+            group, part = divmod(i, CHUNKS)
             if part == 0:
-                conv_sums[pixel] = sums.tile([P, FILTERS], F32, name="conv_sum")
+                conv_sums[group] = sums.tile([P, 512], F32, name="conv_sum")
             for g in range(CHUNK_PASSES):
                 c = part * CHUNK_PASSES + g
+                rows = slice(g * GROUP_ROWS, (g + 1) * GROUP_ROWS)
                 nc.tensor.matmul_mx(
-                    out=conv_sums[pixel][:],
-                    lhsT=code_tiles[i][:, g * P : (g + 1) * P].bitcast(FP8X4),
-                    lhsT_scale=scale_tiles[i][:, g * P : (g + 1) * P],
-                    rhs=w_codes[:, c * FILTERS : (c + 1) * FILTERS].bitcast(FP8X4),
-                    rhs_scale=w_scales[:, c * FILTERS : (c + 1) * FILTERS],
+                    out=conv_sums[group][:, 0:GROUP_ROWS],
+                    lhsT=w_codes[:, c * FILTERS : (c + 1) * FILTERS].bitcast(FP8X4),
+                    lhsT_scale=w_scales[:, c * FILTERS : (c + 1) * FILTERS],
+                    rhs=code_tiles[i][:, rows].bitcast(FP8X4),
+                    rhs_scale=scale_tiles[i][:, rows],
                     start=(c == 0),
                     stop=(c == PASSES - 1),
                 )
 
-        def closes_pixel(i):
-            return 0 <= i < N_CHUNKS and i % CHUNKS_PER_PIXEL == CHUNKS_PER_PIXEL - 1
+        def by_sample(tile):
+            return tile[:].rearrange("n (b q) -> n b q", q=PIXELS)
 
-        relu = keep.tile([P, PIXELS, FILTERS], F32)
-        dev = keep.tile([P, PIXELS, FILTERS], F32)
+        def spread(columns):
+            return columns.unsqueeze(2).to_broadcast([P, GROUP_SAMPLES, PIXELS])
 
-        def add_noise(i):
-            if not closes_pixel(i):
-                return
-            pixel = i // CHUNKS_PER_PIXEL
-            pre_relu[pixel] = work.tile([P, FILTERS], F32, name="pre")
+        def fresh(group, name, width):
+            epilogue[group, name] = work.tile([P, width], F32, name=name)
+            return epilogue[group, name]
+
+        def add_noise(group):
             nc.vector.tensor_tensor(
-                out=pre_relu[pixel][:],
-                in0=conv_sums[pixel][:],
-                in1=noise_bias[:, pixel, :],
+                out=fresh(group, "pre", GROUP_ROWS)[:],
+                in0=conv_sums[group][:, 0:GROUP_ROWS],
+                in1=noise_bias[:, group * GROUP_ROWS : (group + 1) * GROUP_ROWS],
                 op=ALU.add,
             )
 
-        def leaky_relu(i):
-            if not closes_pixel(i):
-                return
-            pixel = i // CHUNKS_PER_PIXEL
+        def leaky_relu(group):
+            pre = epilogue[group, "pre"]
             nc.vector.scalar_tensor_tensor(
-                out=relu[:, pixel, :],
-                in0=pre_relu[pixel][:],
+                out=fresh(group, "relu", GROUP_ROWS)[:],
+                in0=pre[:],
                 scalar=SLOPE,
-                in1=pre_relu[pixel][:],
+                in1=pre[:],
                 op0=ALU.mult,
                 op1=ALU.max,
             )
-            nc.gpsimd.tensor_tensor(
-                out=dev[:, pixel, :], in0=relu[:, pixel, :], in1=relu[:, 0, :], op=ALU.subtract
-            )
-            nc.gpsimd.tensor_tensor(
-                out=dev_sum[:], in0=dev_sum[:], in1=dev[:, pixel, :], op=ALU.add
-            )
 
-        def square(i):
-            if not closes_pixel(i):
-                return
-            pixel = i // CHUNKS_PER_PIXEL
-            squares[pixel] = work.tile([P, FILTERS], F32, name="sq")
-            nc.scalar.activation(out=squares[pixel][:], in_=dev[:, pixel, :], func=ACT.Square)
-            nc.gpsimd.tensor_tensor(out=sq_sum[:], in0=sq_sum[:], in1=squares[pixel][:], op=ALU.add)
-
-        for step in range(N_CHUNKS + 3):
-            add_noise(step - 3)
-            quantise(step - 1)
-            leaky_relu(step - 3)
-            transpose(step)
-            load(step + X_BUFS)
-            multiply(step - 2)
-            square(step - 3)
-
-        mean = keep.tile([P, FILTERS], F32)
-        nc.vector.tensor_scalar_mul(out=mean[:], in0=dev_sum[:], scalar1=1.0 / PIXELS)
-        mean_sq = keep.tile([P, FILTERS], F32)
-        nc.vector.tensor_mul(out=mean_sq[:], in0=mean[:], in1=mean[:])
-        second = keep.tile([P, FILTERS], F32)
-        nc.vector.tensor_scalar(
-            out=second[:],
-            in0=sq_sum[:],
-            scalar1=1.0 / PIXELS,
-            scalar2=EPS,
-            op0=ALU.mult,
-            op1=ALU.add,
-        )
-        var_eps = keep.tile([P, FILTERS], F32)
-        nc.vector.tensor_sub(out=var_eps[:], in0=second[:], in1=mean_sq[:])
-        std = keep.tile([P, FILTERS], F32)
-        nc.scalar.activation(out=std[:], in_=var_eps[:], func=ACT.Sqrt)
-        inv_std = keep.tile([P, FILTERS], F32)
-        nc.vector.reciprocal(out=inv_std[:], in_=std[:])
-        gain = keep.tile([P, FILTERS], F32)
-        nc.vector.tensor_mul(out=gain[:], in0=inv_std[:], in1=gamma1[:])
-        mean_gain = keep.tile([P, FILTERS], F32)
-        nc.vector.tensor_mul(out=mean_gain[:], in0=mean[:], in1=gain[:])
-        shift = keep.tile([P, FILTERS], F32)
-        nc.vector.tensor_sub(out=shift[:], in0=beta[:], in1=mean_gain[:])
-
-        result = keep.tile([P, PIXELS, FILTERS], F32)
-        STORE_PIXELS = 4
-        for first in range(0, PIXELS, STORE_PIXELS):
-            some = slice(first, first + STORE_PIXELS)
-            nc.vector.tensor_tensor(
-                out=result[:, some, :],
-                in0=dev[:, some, :],
-                in1=gain[:].unsqueeze(1).to_broadcast([P, STORE_PIXELS, FILTERS]),
-                op=ALU.mult,
-            )
-        for first in range(0, PIXELS, STORE_PIXELS):
-            some = slice(first, first + STORE_PIXELS)
-            nc.vector.tensor_tensor(
-                out=result[:, some, :],
-                in0=result[:, some, :],
-                in1=shift[:].unsqueeze(1).to_broadcast([P, STORE_PIXELS, FILTERS]),
+        def total(group):
+            nc.vector.tensor_reduce(
+                out=fresh(group, "total", GROUP_SAMPLES)[:],
+                in_=by_sample(epilogue[group, "relu"]),
+                axis=AXIS.X,
                 op=ALU.add,
             )
-            nc.sync.dma_start(out=out_rows[:, some, :], in_=result[:, some, :])
+
+        def centre(group):
+            nc.vector.scalar_tensor_tensor(
+                out=by_sample(fresh(group, "dev", GROUP_ROWS)),
+                in0=by_sample(epilogue[group, "relu"]),
+                scalar=float(PIXELS),
+                in1=spread(epilogue[group, "total"][:]),
+                op0=ALU.mult,
+                op1=ALU.subtract,
+            )
+
+        def square(group):
+            nc.scalar.activation(
+                out=fresh(group, "squares", GROUP_ROWS)[:],
+                in_=epilogue[group, "dev"][:],
+                func=ACT.Square,
+                scale=1.0 / 64.0,
+            )
+
+        def variance(group):
+            nc.vector.tensor_reduce(
+                out=fresh(group, "var", GROUP_SAMPLES)[:],
+                in_=by_sample(epilogue[group, "squares"]),
+                axis=AXIS.X,
+                op=ALU.add,
+            )
+
+        def add_eps(group):
+            nc.vector.tensor_scalar(
+                out=fresh(group, "var256", GROUP_SAMPLES)[:],
+                in0=epilogue[group, "var"][:],
+                scalar1=EPS,
+                scalar2=256.0,
+                op0=ALU.add,
+                op1=ALU.mult,
+            )
+
+        def inverse(group):
+            nc.scalar.activation(
+                out=fresh(group, "inv", GROUP_SAMPLES)[:],
+                in_=epilogue[group, "var256"][:],
+                func=ACT.Abs_reciprocal_sqrt,
+            )
+
+        def samples_of(group):
+            return slice(group * GROUP_SAMPLES, (group + 1) * GROUP_SAMPLES)
+
+        def gain(group):
+            nc.vector.tensor_mul(
+                out=fresh(group, "gain", GROUP_SAMPLES)[:],
+                in0=epilogue[group, "inv"][:],
+                in1=gamma1[:, samples_of(group)],
+            )
+
+        def scale_up(group):
+            nc.vector.tensor_tensor(
+                out=by_sample(fresh(group, "scaled", GROUP_ROWS)),
+                in0=by_sample(epilogue[group, "dev"]),
+                in1=spread(epilogue[group, "gain"][:]),
+                op=ALU.mult,
+            )
+
+        def add_beta(group):
+            nc.vector.tensor_tensor(
+                out=by_sample(fresh(group, "styled", GROUP_ROWS)),
+                in0=by_sample(epilogue[group, "scaled"]),
+                in1=spread(beta[:, samples_of(group)]),
+                op=ALU.add,
+            )
+
+        def turn_back(group):
+            turned = banks.tile([P, TILES, FILTERS], F32, tag="bank", name="turned")
+            for s in range(TILES):
+                nc.tensor.transpose(
+                    turned[:, s, :],
+                    epilogue[group, "styled"][:, s * P : (s + 1) * P],
+                    ident_f32[:],
+                )
+            epilogue[group, "turned"] = turned
+
+        def store(group):
+            result = work.tile([P, TILES, FILTERS], F32, name="result")
+            nc.scalar.copy(out=result[:], in_=epilogue[group, "turned"][:])
+            queue = nc.sync if group == GROUPS - 1 else nc.gpsimd
+            queue.dma_start(out=out_rows[group], in_=result[:])
+
+        VECTOR_PLACES = {
+            (1, 2): add_noise,
+            (2, 0): leaky_relu,
+            (2, 2): total,
+            (3, 0): centre,
+            (3, 2): variance,
+            (4, 0): add_eps,
+            (4, 2): gain,
+            (5, 0): scale_up,
+            (5, 1): add_beta,
+        }
+        SCALAR_PLACES = {(3, 1): square, (4, 0): inverse, (6, 0): store}
+
+        def at(places, step, place):
+            for (after, where), part in places.items():
+                group, rest = divmod(step - 2 - after - (CHUNKS - 1), CHUNKS)
+                if where == place and rest == 0 and 0 <= group < GROUPS:
+                    part(group)
+
+        def scalar_epilogue(step, place):
+            at(SCALAR_PLACES, step, place)
+
+        def vector_epilogue(step, place):
+            at(VECTOR_PLACES, step, place)
+
+        for step in range(STEPS + 9):
+            vector_epilogue(step, 0)
+            sort_words(step + 1, 0)
+            vector_epilogue(step, 1)
+            if step < CHUNKS:
+                group_w(step)
+            quantise(step - 1)
+            if step < CHUNKS:
+                quantise_w(step)
+            if step < STEPS:
+                transpose(step)
+            else:
+                for place in range(CHUNK_PASSES):
+                    scalar_epilogue(step, place)
+                    if place == 1:
+                        vector_epilogue(step, 2)
+            load(step + X_BUFS)
+            multiply(step - 2)
+            if step in (2, 3):
+                noise_table((step - 2) * 1024)
+                noise_table((step - 2) * 1024 + 512)
+            if step == 4:
+                turn_latents()
+            if step == 5:
+                style_table()
+            group, rest = divmod(step - 2 - 5 - (CHUNKS - 1), CHUNKS)
+            if rest == 0 and 0 <= group < GROUPS:
+                turn_back(group)

@@ -34,7 +34,10 @@ CHUNK_COLS = CHUNK_PASSES * K_PASS
 CHUNKS = PASSES // CHUNK_PASSES
 STEPS = GROUPS * CHUNKS
 X_BUFS = 10
-SORTED = (1, 3)
+W_AFTER = (0, 2, 3, 5)
+W_STEPS = (0, 2, 4, 6)
+FIRST_MX_STEPS = (2, 3, 5, 7)
+FIRST_SORTED = 9
 
 FLOPS = 2 * ROWS * CHANNELS * FILTERS + 2 * SAMPLES * LATENT * 2 * FILTERS
 
@@ -50,7 +53,7 @@ def tile_styleganlayerepilogue_k_kernel(
         ctx.enter_context(tc.manual_schedule())
         keep = ctx.enter_context(tc.tile_pool(name="keep", bufs=1))
         x_pool = ctx.enter_context(tc.tile_pool(name="x_pool", bufs=X_BUFS))
-        sorted_pool = ctx.enter_context(tc.tile_pool(name="sorted_pool", bufs=3))
+        sorted_pool = ctx.enter_context(tc.tile_pool(name="sorted_pool", bufs=2))
         grouped_pool = ctx.enter_context(tc.tile_pool(name="grouped_pool", bufs=3))
         codes_pool = ctx.enter_context(tc.tile_pool(name="codes_pool", bufs=3))
         work = ctx.enter_context(tc.tile_pool(name="work", bufs=2))
@@ -64,6 +67,7 @@ def tile_styleganlayerepilogue_k_kernel(
         scale_tiles = {}
         conv_sums = {}
         epilogue = {}
+        style_parts = {}
 
         def load(i):
             if i >= STEPS:
@@ -72,8 +76,9 @@ def tile_styleganlayerepilogue_k_kernel(
             x_chunk = x_pool.tile([P, TILES, CHUNK_COLS], BF16, name="x_chunk")
             cols = slice(part * CHUNK_COLS, (part + 1) * CHUNK_COLS)
             if i == 0:
-                for s in range(TILES):
-                    nc.sync.dma_start(out=x_chunk[:, s, :], in_=x_rows[group, :, s, cols])
+                for g in range(CHUNK_PASSES):
+                    some = slice(g * K_PASS, (g + 1) * K_PASS)
+                    nc.sync.dma_start(out=x_chunk[:, :, some], in_=x_rows[group, :, :, some])
             else:
                 nc.sync.dma_start(out=x_chunk[:], in_=x_rows[group, :, :, cols])
             x_chunks[i] = x_chunk
@@ -113,17 +118,19 @@ def tile_styleganlayerepilogue_k_kernel(
 
         for i in range(X_BUFS):
             load(i)
+            if i in W_AFTER:
+                load_w(W_AFTER.index(i))
             if i == 1:
                 load_noise()
-            if i == 3:
+            if i == 4:
                 load_style()
-            if i < CHUNKS:
-                load_w(i)
 
         ident_f32 = keep.tile([P, P], F32)
         make_identity(nc, ident_f32[:])
         one = keep.tile([P, 1], F32)
         nc.vector.memset(one[:], 1.0)
+        eps256 = keep.tile([P, 1], F32)
+        nc.vector.memset(eps256[:], 256.0 * EPS)
         warm = keep.tile([P, 1], F32)
         nc.scalar.activation(out=warm[:], in_=one[:], func=ACT.Abs_reciprocal_sqrt)
         ident_bf = keep.tile([P, P], BF16)
@@ -151,7 +158,10 @@ def tile_styleganlayerepilogue_k_kernel(
                 nc.tensor.transpose(
                     latents_ps[:, c, :], latents[:, c * P : (c + 1) * P], ident_bf[:]
                 )
-            nc.vector.tensor_copy(out=latents_t[:], in_=latents_ps[:])
+            style_parts["latents"] = latents_ps
+
+        def copy_latents():
+            nc.vector.tensor_copy(out=latents_t[:], in_=style_parts["latents"][:])
 
         def style_table():
             style_ps = banks.tile([P, 2, SAMPLES], F32, tag="bank", name="style_ps")
@@ -172,6 +182,10 @@ def tile_styleganlayerepilogue_k_kernel(
                     start=False,
                     stop=True,
                 )
+            style_parts["style"] = style_ps
+
+        def copy_style():
+            style_ps = style_parts["style"]
             nc.vector.tensor_scalar_add(out=gamma1[:], in0=style_ps[:, 0, :], scalar1=1.0)
             nc.vector.tensor_copy(out=beta[:], in_=style_ps[:, 1, :])
 
@@ -195,14 +209,12 @@ def tile_styleganlayerepilogue_k_kernel(
                 in_=w_grouped[:, passes, :, :].rearrange("p c n t -> p (c n t)"),
             )
 
-        def sorted_passes(i):
-            return SORTED if i >= CHUNKS else ()
-
-        def sort_words(i, which):
-            if i >= STEPS or which >= len(sorted_passes(i)):
+        def sort_words(step, half):
+            i = step + 2 if step % 2 == 1 else step + 1
+            if i >= STEPS or i < FIRST_SORTED:
                 return
-            g = sorted_passes(i)[which]
-            tile = sorted_pool.tile([P, TILES, 2, P], F32, tag="sorted%d" % which, name="in_order")
+            g = half if step % 2 == 1 else 2 + half
+            tile = sorted_pool.tile([P, TILES, 2, P], F32, tag="sorted%d" % g, name="in_order")
             words = x_chunks[i][:, :, g * K_PASS : (g + 1) * K_PASS].bitcast(F32)
             nc.vector.tensor_copy(out=tile[:], in_=words.rearrange("p s (r u) -> p s u r", u=2))
             sorted_words[i, g] = tile
@@ -212,6 +224,7 @@ def tile_styleganlayerepilogue_k_kernel(
             grouped = grouped_pool.tile(
                 [P, CHUNK_PASSES, GROUP_ROWS * PACK], BF16, align_bytes=64, name="grouped"
             )
+            grouped_tiles[i] = grouped
             for g in range(CHUNK_PASSES):
                 xt = banks.tile([P, TILES, 2, P], F32, tag="bank", name="xt")
                 for s in range(TILES):
@@ -228,25 +241,44 @@ def tile_styleganlayerepilogue_k_kernel(
                 scalar_epilogue(i, g)
                 if g == 1:
                     vector_epilogue(i, 2)
-                    sort_words(i + 1, 1)
-            grouped_tiles[i] = grouped
+                    sort_words(i, 1)
+                if i == STEPS - 1:
+                    quantise_pass(i, g)
+
+        def code_room(i):
+            code_tiles[i] = codes_pool.tile(
+                [P, CHUNK_PASSES * GROUP_ROWS], U32, align_bytes=64, name="codes"
+            )
+            scale_tiles[i] = codes_pool.tile(
+                [P, CHUNK_PASSES * GROUP_ROWS], U8, align_bytes=64, name="scales"
+            )
 
         def quantise(i):
-            if i < 0 or i >= STEPS:
+            if i < 0 or i >= STEPS - 1:
                 return
-            codes = codes_pool.tile([P, CHUNK_PASSES * GROUP_ROWS], U32, align_bytes=64, name="codes")
-            scales = codes_pool.tile([P, CHUNK_PASSES * GROUP_ROWS], U8, align_bytes=64, name="scales")
+            code_room(i)
             nc.vector.quantize_mx(
-                out=codes[:].bitcast(FP8X4),
-                scales=scales[:],
+                out=code_tiles[i][:].bitcast(FP8X4),
+                scales=scale_tiles[i][:],
                 in_=grouped_tiles[i][:].rearrange("p c r -> p (c r)"),
             )
-            code_tiles[i] = codes
-            scale_tiles[i] = scales
+
+        def quantise_pass(i, g):
+            if g == 0:
+                code_room(i)
+            rows = slice(g * GROUP_ROWS, (g + 1) * GROUP_ROWS)
+            nc.vector.quantize_mx(
+                out=code_tiles[i][:, rows].bitcast(FP8X4),
+                scales=scale_tiles[i][:, rows],
+                in_=grouped_tiles[i][:, g, :],
+            )
+
+        def mx_step(i):
+            if i < CHUNKS:
+                return FIRST_MX_STEPS[i]
+            return i + 1 if i == STEPS - 1 else i + 2
 
         def multiply(i):
-            if i < 0 or i >= STEPS:
-                return
             group, part = divmod(i, CHUNKS)
             if part == 0:
                 conv_sums[group] = sums.tile([P, 512], F32, name="conv_sum")
@@ -263,28 +295,46 @@ def tile_styleganlayerepilogue_k_kernel(
                     stop=(c == PASSES - 1),
                 )
 
+        def units(group):
+            if group < GROUPS - 1:
+                return [(group, 0, GROUP_SAMPLES)]
+            half = GROUP_SAMPLES // 2
+            return [(group, 0, half), (group, half, half)]
+
+        def rows_of(unit):
+            return slice(unit[1] * PIXELS, (unit[1] + unit[2]) * PIXELS)
+
+        def samples_of(unit):
+            first = unit[0] * GROUP_SAMPLES + unit[1]
+            return slice(first, first + unit[2])
+
         def by_sample(tile):
             return tile[:].rearrange("n (b q) -> n b q", q=PIXELS)
 
-        def spread(columns):
-            return columns.unsqueeze(2).to_broadcast([P, GROUP_SAMPLES, PIXELS])
+        def spread(unit, columns):
+            return columns.unsqueeze(2).to_broadcast([P, unit[2], PIXELS])
 
-        def fresh(group, name, width):
-            epilogue[group, name] = work.tile([P, width], F32, name=name)
-            return epilogue[group, name]
+        def pixel_tile(unit, name):
+            epilogue[unit, name] = work.tile([P, unit[2] * PIXELS], F32, name=name)
+            return epilogue[unit, name]
 
-        def add_noise(group):
+        def sample_tile(unit, name):
+            epilogue[unit, name] = work.tile([P, unit[2]], F32, name=name)
+            return epilogue[unit, name]
+
+        def add_noise(unit):
+            first = unit[0] * GROUP_ROWS + unit[1] * PIXELS
             nc.vector.tensor_tensor(
-                out=fresh(group, "pre", GROUP_ROWS)[:],
-                in0=conv_sums[group][:, 0:GROUP_ROWS],
-                in1=noise_bias[:, group * GROUP_ROWS : (group + 1) * GROUP_ROWS],
+                out=pixel_tile(unit, "pre")[:],
+                in0=conv_sums[unit[0]][:, rows_of(unit)],
+                in1=noise_bias[:, first : first + unit[2] * PIXELS],
                 op=ALU.add,
             )
 
-        def leaky_relu(group):
-            pre = epilogue[group, "pre"]
+        def leaky_relu(unit):
+            pre = epilogue[unit, "pre"]
             nc.vector.scalar_tensor_tensor(
-                out=fresh(group, "relu", GROUP_ROWS)[:],
+                out=pixel_tile(unit, "relu")[:],
                 in0=pre[:],
                 scalar=SLOPE,
                 in1=pre[:],
@@ -292,117 +342,111 @@ def tile_styleganlayerepilogue_k_kernel(
                 op1=ALU.max,
             )
 
-        def total(group):
+        def total(unit):
             nc.vector.tensor_reduce(
-                out=fresh(group, "total", GROUP_SAMPLES)[:],
-                in_=by_sample(epilogue[group, "relu"]),
+                out=sample_tile(unit, "total")[:],
+                in_=by_sample(epilogue[unit, "relu"]),
                 axis=AXIS.X,
                 op=ALU.add,
             )
 
-        def centre(group):
+        def centre(unit):
             nc.vector.scalar_tensor_tensor(
-                out=by_sample(fresh(group, "dev", GROUP_ROWS)),
-                in0=by_sample(epilogue[group, "relu"]),
+                out=by_sample(pixel_tile(unit, "dev")),
+                in0=by_sample(epilogue[unit, "relu"]),
                 scalar=float(PIXELS),
-                in1=spread(epilogue[group, "total"][:]),
+                in1=spread(unit, epilogue[unit, "total"][:]),
                 op0=ALU.mult,
                 op1=ALU.subtract,
             )
 
-        def square(group):
+        def square(unit):
             nc.scalar.activation(
-                out=fresh(group, "squares", GROUP_ROWS)[:],
-                in_=epilogue[group, "dev"][:],
+                out=pixel_tile(unit, "squares")[:],
+                in_=epilogue[unit, "dev"][:],
                 func=ACT.Square,
                 scale=1.0 / 64.0,
             )
 
-        def variance(group):
+        def variance(unit):
             nc.vector.tensor_reduce(
-                out=fresh(group, "var", GROUP_SAMPLES)[:],
-                in_=by_sample(epilogue[group, "squares"]),
+                out=sample_tile(unit, "var")[:],
+                in_=by_sample(epilogue[unit, "squares"]),
                 axis=AXIS.X,
                 op=ALU.add,
             )
 
-        def add_eps(group):
-            nc.vector.tensor_scalar(
-                out=fresh(group, "var256", GROUP_SAMPLES)[:],
-                in0=epilogue[group, "var"][:],
-                scalar1=EPS,
-                scalar2=256.0,
-                op0=ALU.add,
-                op1=ALU.mult,
-            )
-
-        def inverse(group):
+        def inverse(unit):
             nc.scalar.activation(
-                out=fresh(group, "inv", GROUP_SAMPLES)[:],
-                in_=epilogue[group, "var256"][:],
+                out=sample_tile(unit, "inv")[:],
+                in_=epilogue[unit, "var"][:],
                 func=ACT.Abs_reciprocal_sqrt,
+                scale=256.0,
+                bias=eps256[:],
             )
 
-        def samples_of(group):
-            return slice(group * GROUP_SAMPLES, (group + 1) * GROUP_SAMPLES)
-
-        def gain(group):
+        def gain(unit):
             nc.vector.tensor_mul(
-                out=fresh(group, "gain", GROUP_SAMPLES)[:],
-                in0=epilogue[group, "inv"][:],
-                in1=gamma1[:, samples_of(group)],
+                out=sample_tile(unit, "gain")[:],
+                in0=epilogue[unit, "inv"][:],
+                in1=gamma1[:, samples_of(unit)],
             )
 
-        def scale_up(group):
+        def scale_up(unit):
             nc.vector.tensor_tensor(
-                out=by_sample(fresh(group, "scaled", GROUP_ROWS)),
-                in0=by_sample(epilogue[group, "dev"]),
-                in1=spread(epilogue[group, "gain"][:]),
+                out=by_sample(pixel_tile(unit, "scaled")),
+                in0=by_sample(epilogue[unit, "dev"]),
+                in1=spread(unit, epilogue[unit, "gain"][:]),
                 op=ALU.mult,
             )
 
-        def add_beta(group):
+        def add_beta(unit):
             nc.vector.tensor_tensor(
-                out=by_sample(fresh(group, "styled", GROUP_ROWS)),
-                in0=by_sample(epilogue[group, "scaled"]),
-                in1=spread(beta[:, samples_of(group)]),
+                out=by_sample(pixel_tile(unit, "styled")),
+                in0=by_sample(epilogue[unit, "scaled"]),
+                in1=spread(unit, beta[:, samples_of(unit)]),
                 op=ALU.add,
             )
 
-        def turn_back(group):
-            turned = banks.tile([P, TILES, FILTERS], F32, tag="bank", name="turned")
-            for s in range(TILES):
+        def turn_back(unit):
+            tiles = unit[2] * PIXELS // P
+            turned = banks.tile([P, tiles, FILTERS], F32, tag="bank", name="turned")
+            for s in range(tiles):
                 nc.tensor.transpose(
                     turned[:, s, :],
-                    epilogue[group, "styled"][:, s * P : (s + 1) * P],
+                    epilogue[unit, "styled"][:, s * P : (s + 1) * P],
                     ident_f32[:],
                 )
-            epilogue[group, "turned"] = turned
+            epilogue[unit, "turned"] = turned
 
-        def store(group):
-            result = work.tile([P, TILES, FILTERS], F32, name="result")
-            nc.scalar.copy(out=result[:], in_=epilogue[group, "turned"][:])
-            queue = nc.sync if group == GROUPS - 1 else nc.gpsimd
-            queue.dma_start(out=out_rows[group], in_=result[:])
+        def store(unit):
+            first = unit[1] * PIXELS // P
+            tiles = unit[2] * PIXELS // P
+            result = work.tile([P, tiles, FILTERS], F32, name="result")
+            nc.scalar.copy(out=result[:], in_=epilogue[unit, "turned"][:])
+            queue = nc.sync if unit[0] == GROUPS - 1 else nc.gpsimd
+            queue.dma_start(out=out_rows[unit[0], :, first : first + tiles, :], in_=result[:])
 
         VECTOR_PLACES = {
-            (1, 2): add_noise,
-            (2, 0): leaky_relu,
-            (2, 2): total,
-            (3, 0): centre,
-            (3, 2): variance,
-            (4, 0): add_eps,
-            (4, 2): gain,
-            (5, 0): scale_up,
-            (5, 1): add_beta,
+            (1, 1): add_noise,
+            (1, 2): leaky_relu,
+            (2, 0): total,
+            (2, 1): centre,
+            (3, 0): variance,
+            (3, 2): gain,
+            (4, 0): scale_up,
+            (4, 1): add_beta,
         }
-        SCALAR_PLACES = {(3, 1): square, (4, 0): inverse, (6, 0): store}
+        SCALAR_PLACES = {(2, 1): square, (3, 0): inverse, (5, 0): store}
+        TENSOR_PLACES = {(4, 0): turn_back}
 
         def at(places, step, place):
             for (after, where), part in places.items():
-                group, rest = divmod(step - 2 - after - (CHUNKS - 1), CHUNKS)
-                if where == place and rest == 0 and 0 <= group < GROUPS:
-                    part(group)
+                for group in range(GROUPS):
+                    last_pass = mx_step(group * CHUNKS + CHUNKS - 1)
+                    if where == place and last_pass + after == step:
+                        for unit in units(group):
+                            part(unit)
 
         def scalar_epilogue(step, place):
             at(SCALAR_PLACES, step, place)
@@ -410,15 +454,18 @@ def tile_styleganlayerepilogue_k_kernel(
         def vector_epilogue(step, place):
             at(VECTOR_PLACES, step, place)
 
-        for step in range(STEPS + 9):
+        for step in range(STEPS + 7):
             vector_epilogue(step, 0)
-            sort_words(step + 1, 0)
+            sort_words(step, 0)
             vector_epilogue(step, 1)
-            if step < CHUNKS:
-                group_w(step)
             quantise(step - 1)
-            if step < CHUNKS:
-                quantise_w(step)
+            if step == 8:
+                copy_latents()
+            if step == 9:
+                copy_style()
+            if step in W_STEPS:
+                group_w(W_STEPS.index(step))
+                quantise_w(W_STEPS.index(step))
             if step < STEPS:
                 transpose(step)
             else:
@@ -427,14 +474,13 @@ def tile_styleganlayerepilogue_k_kernel(
                     if place == 1:
                         vector_epilogue(step, 2)
             load(step + X_BUFS)
-            multiply(step - 2)
-            if step in (2, 3):
-                noise_table((step - 2) * 1024)
-                noise_table((step - 2) * 1024 + 512)
-            if step == 4:
+            for i in range(STEPS):
+                if mx_step(i) == step:
+                    multiply(i)
+            if 2 <= step < 6:
+                noise_table((step - 2) * 512)
+            if step == 7:
                 turn_latents()
-            if step == 5:
+            if step == 8:
                 style_table()
-            group, rest = divmod(step - 2 - 5 - (CHUNKS - 1), CHUNKS)
-            if rest == 0 and 0 <= group < GROUPS:
-                turn_back(group)
+            at(TENSOR_PLACES, step, 0)

@@ -37,7 +37,8 @@ X_BUFS = 10
 W_AFTER = (0, 2, 3, 5)
 W_STEPS = (0, 2, 4, 6)
 FIRST_MX_STEPS = (2, 3, 5, 7)
-FIRST_SORTED = 9
+FIRST_SORTED = 11
+FIRST_AHEAD = 15
 
 FLOPS = 2 * ROWS * CHANNELS * FILTERS + 2 * SAMPLES * LATENT * 2 * FILTERS
 
@@ -57,6 +58,7 @@ def tile_styleganlayerepilogue_k_kernel(
         grouped_pool = ctx.enter_context(tc.tile_pool(name="grouped_pool", bufs=3))
         codes_pool = ctx.enter_context(tc.tile_pool(name="codes_pool", bufs=3))
         work = ctx.enter_context(tc.tile_pool(name="work", bufs=2))
+        result_pool = ctx.enter_context(tc.tile_pool(name="result_pool", bufs=4))
         banks = ctx.enter_context(tc.psum_pool(name="banks", bufs=6))
         sums = ctx.enter_context(tc.psum_pool(name="sums", bufs=2))
 
@@ -209,15 +211,23 @@ def tile_styleganlayerepilogue_k_kernel(
                 in_=w_grouped[:, passes, :, :].rearrange("p c n t -> p (c n t)"),
             )
 
-        def sort_words(step, half):
-            i = step + 2 if step % 2 == 1 else step + 1
-            if i >= STEPS or i < FIRST_SORTED:
-                return
-            g = half if step % 2 == 1 else 2 + half
-            tile = sorted_pool.tile([P, TILES, 2, P], F32, tag="sorted%d" % g, name="in_order")
-            words = x_chunks[i][:, :, g * K_PASS : (g + 1) * K_PASS].bitcast(F32)
-            nc.vector.tensor_copy(out=tile[:], in_=words.rearrange("p s (r u) -> p s u r", u=2))
-            sorted_words[i, g] = tile
+        sorts = {}
+        for i in range(FIRST_SORTED, STEPS, 2):
+            if i < FIRST_AHEAD:
+                sorts[i - 1, 0] = [(i, 0), (i, 1)]
+                sorts[i - 1, 1] = [(i, 2), (i, 3)]
+            else:
+                sorts[i - 2, 0] = [(i, 0)]
+                sorts[i - 2, 1] = [(i, 1)]
+                sorts[i - 1, 0] = [(i, 2)]
+                sorts[i - 1, 1] = [(i, 3)]
+
+        def sort_words(step, place):
+            for i, g in sorts.get((step, place), []):
+                tile = sorted_pool.tile([P, TILES, 2, P], F32, tag="sorted%d" % g, name="in_order")
+                words = x_chunks[i][:, :, g * K_PASS : (g + 1) * K_PASS].bitcast(F32)
+                nc.vector.tensor_copy(out=tile[:], in_=words.rearrange("p s (r u) -> p s u r", u=2))
+                sorted_words[i, g] = tile
 
         def transpose(i):
             words = x_chunks[i][:].bitcast(F32)
@@ -422,7 +432,7 @@ def tile_styleganlayerepilogue_k_kernel(
         def store(unit):
             first = unit[1] * PIXELS // P
             tiles = unit[2] * PIXELS // P
-            result = work.tile([P, tiles, FILTERS], F32, name="result")
+            result = result_pool.tile([P, tiles, FILTERS], F32, name="result")
             nc.scalar.copy(out=result[:], in_=epilogue[unit, "turned"][:])
             queue = nc.sync if unit[0] == GROUPS - 1 else nc.gpsimd
             queue.dma_start(out=out_rows[unit[0], :, first : first + tiles, :], in_=result[:])
@@ -444,7 +454,8 @@ def tile_styleganlayerepilogue_k_kernel(
             for (after, where), part in places.items():
                 for group in range(GROUPS):
                     last_pass = mx_step(group * CHUNKS + CHUNKS - 1)
-                    if where == place and last_pass + after == step:
+                    late = 1 if group == GROUPS - 2 and after > 2 else 0
+                    if where == place and last_pass + after + late == step:
                         for unit in units(group):
                             part(unit)
 
@@ -454,7 +465,7 @@ def tile_styleganlayerepilogue_k_kernel(
         def vector_epilogue(step, place):
             at(VECTOR_PLACES, step, place)
 
-        for step in range(STEPS + 7):
+        for step in range(STEPS + 8):
             vector_epilogue(step, 0)
             sort_words(step, 0)
             vector_epilogue(step, 1)

@@ -434,8 +434,7 @@ def tile_styleganlayerepilogue_k_kernel(
             tiles = unit[2] * PIXELS // P
             result = result_pool.tile([P, tiles, FILTERS], F32, name="result")
             nc.scalar.copy(out=result[:], in_=epilogue[unit, "turned"][:])
-            queue = nc.sync if unit[0] == GROUPS - 1 else nc.gpsimd
-            queue.dma_start(out=out_rows[unit[0], :, first : first + tiles, :], in_=result[:])
+            nc.sync.dma_start(out=out_rows[unit[0], :, first : first + tiles, :], in_=result[:])
 
         VECTOR_PLACES = {
             (1, 1): add_noise,

from contextlib import ExitStack

import concourse.mybir as mybir
from concourse.masks import make_identity

F32 = mybir.dt.float32
BF16 = mybir.dt.bfloat16
U32 = mybir.dt.uint32
U8 = mybir.dt.uint8
FP8X4 = mybir.dt.float8_e4m3fn_x4
ALU = mybir.AluOpType
ACT = mybir.ActivationFunctionType
AXIS = mybir.AxisListType

P = 128
SAMPLES = 128
PIXELS = 16
ROWS = SAMPLES * PIXELS
CHANNELS = 8192
FILTERS = 128
LATENT = 512
EPS = 1e-8
SLOPE = 0.2

PACK = 4
K_PASS = P * PACK
PASSES = CHANNELS // K_PASS
TILES = 2
GROUP_ROWS = TILES * P
GROUP_SAMPLES = GROUP_ROWS // PIXELS
GROUPS = ROWS // GROUP_ROWS
CHUNK_PASSES = 4
CHUNK_COLS = CHUNK_PASSES * K_PASS
CHUNKS = PASSES // CHUNK_PASSES
STEPS = GROUPS * CHUNKS
X_BUFS = 10
W_AFTER = (0, 2, 3, 5)
W_STEPS = (0, 2, 4, 6)
FIRST_MX_STEPS = (2, 3, 5, 7)
FIRST_SORTED = 11
FIRST_AHEAD = 15

FLOPS = 2 * ROWS * CHANNELS * FILTERS + 2 * SAMPLES * LATENT * 2 * FILTERS


def tile_styleganlayerepilogue_k_kernel(
    tc, x, dlatents, noise_map, conv_w, noise_weight, bias, dense_w, dense_b, out
):
    nc = tc.nc
    x_rows = x.rearrange("b h w c -> (b h w) c").rearrange("(g s p) c -> g p s c", s=TILES, p=P)
    out_rows = out.rearrange("b h w n -> (b h w) n").rearrange("(g s p) n -> g p s n", s=TILES, p=P)

    with ExitStack() as ctx:
        ctx.enter_context(tc.manual_schedule())
        keep = ctx.enter_context(tc.tile_pool(name="keep", bufs=1))
        x_pool = ctx.enter_context(tc.tile_pool(name="x_pool", bufs=X_BUFS))
        sorted_pool = ctx.enter_context(tc.tile_pool(name="sorted_pool", bufs=2))
        grouped_pool = ctx.enter_context(tc.tile_pool(name="grouped_pool", bufs=3))
        codes_pool = ctx.enter_context(tc.tile_pool(name="codes_pool", bufs=3))
        work = ctx.enter_context(tc.tile_pool(name="work", bufs=2))
        result_pool = ctx.enter_context(tc.tile_pool(name="result_pool", bufs=4))
        banks = ctx.enter_context(tc.psum_pool(name="banks", bufs=6))
        sums = ctx.enter_context(tc.psum_pool(name="sums", bufs=2))

        x_chunks = {}
        sorted_words = {}
        grouped_tiles = {}
        code_tiles = {}
        scale_tiles = {}
        conv_sums = {}
        epilogue = {}
        style_parts = {}

        def load(i):
            if i >= STEPS:
                return
            group, part = divmod(i, CHUNKS)
            x_chunk = x_pool.tile([P, TILES, CHUNK_COLS], BF16, name="x_chunk")
            cols = slice(part * CHUNK_COLS, (part + 1) * CHUNK_COLS)
            if i == 0:
                for g in range(CHUNK_PASSES):
                    some = slice(g * K_PASS, (g + 1) * K_PASS)
                    nc.sync.dma_start(out=x_chunk[:, :, some], in_=x_rows[group, :, :, some])
            else:
                nc.sync.dma_start(out=x_chunk[:], in_=x_rows[group, :, :, cols])
            x_chunks[i] = x_chunk

        w_raw = keep.tile([P, PASSES, PACK, FILTERS], BF16)
        w_view = conv_w.rearrange("(c p t) n -> p c (t n)", p=P, t=PACK)

        def load_w(part):
            passes = slice(part * CHUNK_PASSES, (part + 1) * CHUNK_PASSES)
            nc.sync.dma_start(
                out=w_raw[:, passes, :, :].rearrange("p c t n -> p c (t n)"),
                in_=w_view[:, passes, :],
            )

        vectors = keep.tile([P, FILTERS], BF16)
        nc.vector.memset(vectors[:], 0.0)
        noise_rows = keep.tile([P, ROWS], BF16)
        nc.vector.memset(noise_rows[:], 1.0)
        dense_rows = keep.tile([P, 2 * FILTERS], BF16)
        nc.vector.memset(dense_rows[:], 0.0)
        latents = keep.tile([P, LATENT], BF16)
        dense = keep.tile([P, LATENT // P, 2 * FILTERS], BF16)

        def load_noise():
            nc.sync.dma_start(
                out=noise_rows[0:1, :], in_=noise_map.rearrange("b h w o -> o (b h w)")
            )
            nc.sync.dma_start(
                out=vectors[0:1, :], in_=noise_weight.rearrange("a b c n -> (a b c) n")
            )
            nc.sync.dma_start(out=vectors[1:2, :], in_=bias.rearrange("a b c n -> (a b c) n"))

        def load_style():
            nc.sync.dma_start(out=latents[:], in_=dlatents)
            nc.sync.dma_start(out=dense[:], in_=dense_w.rearrange("(c p) n -> p c n", p=P))
            nc.sync.dma_start(out=dense_rows[0:1, :], in_=dense_b.rearrange("(o n) -> o n", o=1))

        for i in range(X_BUFS):
            load(i)
            if i in W_AFTER:
                load_w(W_AFTER.index(i))
            if i == 1:
                load_noise()
            if i == 4:
                load_style()

        ident_f32 = keep.tile([P, P], F32)
        make_identity(nc, ident_f32[:])
        one = keep.tile([P, 1], F32)
        nc.vector.memset(one[:], 1.0)
        eps256 = keep.tile([P, 1], F32)
        nc.vector.memset(eps256[:], 256.0 * EPS)
        warm = keep.tile([P, 1], F32)
        nc.scalar.activation(out=warm[:], in_=one[:], func=ACT.Abs_reciprocal_sqrt)
        ident_bf = keep.tile([P, P], BF16)
        make_identity(nc, ident_bf[:])

        ones = keep.tile([P, SAMPLES], BF16)
        nc.vector.memset(ones[:], 1.0)

        noise_bias = keep.tile([P, ROWS], F32)
        latents_t = keep.tile([P, LATENT // P, SAMPLES], BF16)
        gamma1 = keep.tile([P, SAMPLES], F32)
        beta = keep.tile([P, SAMPLES], F32)

        def noise_table(first):
            cols = slice(first, first + 512)
            noise_ps = banks.tile([P, 512], F32, tag="bank", name="noise_ps")
            nc.tensor.matmul(
                out=noise_ps[:], lhsT=vectors[:], rhs=noise_rows[:, cols], start=True, stop=True
            )
            nc.scalar.copy(out=noise_bias[:, cols], in_=noise_ps[:])

        def turn_latents():
            latents_ps = banks.tile([P, LATENT // P, SAMPLES], BF16, tag="bank", name="latents_ps")
            for c in range(LATENT // P):
                nc.tensor.transpose(
                    latents_ps[:, c, :], latents[:, c * P : (c + 1) * P], ident_bf[:]
                )
            style_parts["latents"] = latents_ps

        def copy_latents():
            nc.vector.tensor_copy(out=latents_t[:], in_=style_parts["latents"][:])

        def style_table():
            style_ps = banks.tile([P, 2, SAMPLES], F32, tag="bank", name="style_ps")
            for half in range(2):
                cols = slice(half * FILTERS, (half + 1) * FILTERS)
                for c in range(LATENT // P):
                    nc.tensor.matmul(
                        out=style_ps[:, half, :],
                        lhsT=dense[:, c, cols],
                        rhs=latents_t[:, c, :],
                        start=(c == 0),
                        stop=False,
                    )
                nc.tensor.matmul(
                    out=style_ps[:, half, :],
                    lhsT=dense_rows[:, cols],
                    rhs=ones[:],
                    start=False,
                    stop=True,
                )
            style_parts["style"] = style_ps

        def copy_style():
            style_ps = style_parts["style"]
            nc.vector.tensor_scalar_add(out=gamma1[:], in0=style_ps[:, 0, :], scalar1=1.0)
            nc.vector.tensor_copy(out=beta[:], in_=style_ps[:, 1, :])

        w_grouped = keep.tile([P, PASSES, FILTERS, PACK], BF16, align_bytes=64)
        w_codes = keep.tile([P, PASSES * FILTERS], U32, align_bytes=64)
        w_scales = keep.tile([P, PASSES * FILTERS], U8, align_bytes=64)

        def group_w(part):
            passes = slice(part * CHUNK_PASSES, (part + 1) * CHUNK_PASSES)
            nc.vector.tensor_copy(
                out=w_grouped[:, passes, :, :],
                in_=w_raw[:, passes, :, :].rearrange("p c t n -> p c n t"),
            )

        def quantise_w(part):
            passes = slice(part * CHUNK_PASSES, (part + 1) * CHUNK_PASSES)
            cols = slice(part * CHUNK_PASSES * FILTERS, (part + 1) * CHUNK_PASSES * FILTERS)
            nc.vector.quantize_mx(
                out=w_codes[:, cols].bitcast(FP8X4),
                scales=w_scales[:, cols],
                in_=w_grouped[:, passes, :, :].rearrange("p c n t -> p (c n t)"),
            )

        sorts = {}
        for i in range(FIRST_SORTED, STEPS, 2):
            if i < FIRST_AHEAD:
                sorts[i - 1, 0] = [(i, 0), (i, 1)]
                sorts[i - 1, 1] = [(i, 2), (i, 3)]
            else:
                sorts[i - 2, 0] = [(i, 0)]
                sorts[i - 2, 1] = [(i, 1)]
                sorts[i - 1, 0] = [(i, 2)]
                sorts[i - 1, 1] = [(i, 3)]

        def sort_words(step, place):
            for i, g in sorts.get((step, place), []):
                tile = sorted_pool.tile([P, TILES, 2, P], F32, tag="sorted%d" % g, name="in_order")
                words = x_chunks[i][:, :, g * K_PASS : (g + 1) * K_PASS].bitcast(F32)
                nc.vector.tensor_copy(out=tile[:], in_=words.rearrange("p s (r u) -> p s u r", u=2))
                sorted_words[i, g] = tile

        def transpose(i):
            words = x_chunks[i][:].bitcast(F32)
            grouped = grouped_pool.tile(
                [P, CHUNK_PASSES, GROUP_ROWS * PACK], BF16, align_bytes=64, name="grouped"
            )
            grouped_tiles[i] = grouped
            for g in range(CHUNK_PASSES):
                xt = banks.tile([P, TILES, 2, P], F32, tag="bank", name="xt")
                for s in range(TILES):
                    for u in range(2):
                        if (i, g) in sorted_words:
                            source = sorted_words[i, g][:, s, u, :]
                        else:
                            source = words[:, s, g * 2 * P + u : (g + 1) * 2 * P : 2]
                        nc.tensor.transpose(xt[:, s, u, :], source, ident_f32[:])
                nc.scalar.copy(
                    out=grouped[:, g, :].bitcast(F32).rearrange("p (s r u) -> p s r u", s=TILES, u=2),
                    in_=xt[:].rearrange("p s u r -> p s r u"),
                )
                scalar_epilogue(i, g)
                if g == 1:
                    vector_epilogue(i, 2)
                    sort_words(i, 1)
                if i == STEPS - 1:
                    quantise_pass(i, g)

        def code_room(i):
            code_tiles[i] = codes_pool.tile(
                [P, CHUNK_PASSES * GROUP_ROWS], U32, align_bytes=64, name="codes"
            )
            scale_tiles[i] = codes_pool.tile(
                [P, CHUNK_PASSES * GROUP_ROWS], U8, align_bytes=64, name="scales"
            )

        def quantise(i):
            if i < 0 or i >= STEPS - 1:
                return
            code_room(i)
            nc.vector.quantize_mx(
                out=code_tiles[i][:].bitcast(FP8X4),
                scales=scale_tiles[i][:],
                in_=grouped_tiles[i][:].rearrange("p c r -> p (c r)"),
            )

        def quantise_pass(i, g):
            if g == 0:
                code_room(i)
            rows = slice(g * GROUP_ROWS, (g + 1) * GROUP_ROWS)
            nc.vector.quantize_mx(
                out=code_tiles[i][:, rows].bitcast(FP8X4),
                scales=scale_tiles[i][:, rows],
                in_=grouped_tiles[i][:, g, :],
            )

        def mx_step(i):
            if i < CHUNKS:
                return FIRST_MX_STEPS[i]
            return i + 1 if i == STEPS - 1 else i + 2

        def multiply(i):
            group, part = divmod(i, CHUNKS)
            if part == 0:
                conv_sums[group] = sums.tile([P, 512], F32, name="conv_sum")
            for g in range(CHUNK_PASSES):
                c = part * CHUNK_PASSES + g
                rows = slice(g * GROUP_ROWS, (g + 1) * GROUP_ROWS)
                nc.tensor.matmul_mx(
                    out=conv_sums[group][:, 0:GROUP_ROWS],
                    lhsT=w_codes[:, c * FILTERS : (c + 1) * FILTERS].bitcast(FP8X4),
                    lhsT_scale=w_scales[:, c * FILTERS : (c + 1) * FILTERS],
                    rhs=code_tiles[i][:, rows].bitcast(FP8X4),
                    rhs_scale=scale_tiles[i][:, rows],
                    start=(c == 0),
                    stop=(c == PASSES - 1),
                )

        def units(group):
            if group < GROUPS - 1:
                return [(group, 0, GROUP_SAMPLES)]
            half = GROUP_SAMPLES // 2
            return [(group, 0, half), (group, half, half)]

        def rows_of(unit):
            return slice(unit[1] * PIXELS, (unit[1] + unit[2]) * PIXELS)

        def samples_of(unit):
            first = unit[0] * GROUP_SAMPLES + unit[1]
            return slice(first, first + unit[2])

        def by_sample(tile):
            return tile[:].rearrange("n (b q) -> n b q", q=PIXELS)

        def spread(unit, columns):
            return columns.unsqueeze(2).to_broadcast([P, unit[2], PIXELS])

        def pixel_tile(unit, name):
            epilogue[unit, name] = work.tile([P, unit[2] * PIXELS], F32, name=name)
            return epilogue[unit, name]

        def sample_tile(unit, name):
            epilogue[unit, name] = work.tile([P, unit[2]], F32, name=name)
            return epilogue[unit, name]

        def add_noise(unit):
            first = unit[0] * GROUP_ROWS + unit[1] * PIXELS
            nc.vector.tensor_tensor(
                out=pixel_tile(unit, "pre")[:],
                in0=conv_sums[unit[0]][:, rows_of(unit)],
                in1=noise_bias[:, first : first + unit[2] * PIXELS],
                op=ALU.add,
            )

        def leaky_relu(unit):
            pre = epilogue[unit, "pre"]
            nc.vector.scalar_tensor_tensor(
                out=pixel_tile(unit, "relu")[:],
                in0=pre[:],
                scalar=SLOPE,
                in1=pre[:],
                op0=ALU.mult,
                op1=ALU.max,
            )

        def total(unit):
            nc.vector.tensor_reduce(
                out=sample_tile(unit, "total")[:],
                in_=by_sample(epilogue[unit, "relu"]),
                axis=AXIS.X,
                op=ALU.add,
            )

        def centre(unit):
            nc.vector.scalar_tensor_tensor(
                out=by_sample(pixel_tile(unit, "dev")),
                in0=by_sample(epilogue[unit, "relu"]),
                scalar=float(PIXELS),
                in1=spread(unit, epilogue[unit, "total"][:]),
                op0=ALU.mult,
                op1=ALU.subtract,
            )

        def square(unit):
            nc.scalar.activation(
                out=pixel_tile(unit, "squares")[:],
                in_=epilogue[unit, "dev"][:],
                func=ACT.Square,
                scale=1.0 / 64.0,
            )

        def variance(unit):
            nc.vector.tensor_reduce(
                out=sample_tile(unit, "var")[:],
                in_=by_sample(epilogue[unit, "squares"]),
                axis=AXIS.X,
                op=ALU.add,
            )

        def inverse(unit):
            nc.scalar.activation(
                out=sample_tile(unit, "inv")[:],
                in_=epilogue[unit, "var"][:],
                func=ACT.Abs_reciprocal_sqrt,
                scale=256.0,
                bias=eps256[:],
            )

        def gain(unit):
            nc.vector.tensor_mul(
                out=sample_tile(unit, "gain")[:],
                in0=epilogue[unit, "inv"][:],
                in1=gamma1[:, samples_of(unit)],
            )

        def scale_up(unit):
            nc.vector.tensor_tensor(
                out=by_sample(pixel_tile(unit, "scaled")),
                in0=by_sample(epilogue[unit, "dev"]),
                in1=spread(unit, epilogue[unit, "gain"][:]),
                op=ALU.mult,
            )

        def add_beta(unit):
            nc.vector.tensor_tensor(
                out=by_sample(pixel_tile(unit, "styled")),
                in0=by_sample(epilogue[unit, "scaled"]),
                in1=spread(unit, beta[:, samples_of(unit)]),
                op=ALU.add,
            )

        def turn_back(unit):
            tiles = unit[2] * PIXELS // P
            turned = banks.tile([P, tiles, FILTERS], F32, tag="bank", name="turned")
            for s in range(tiles):
                nc.tensor.transpose(
                    turned[:, s, :],
                    epilogue[unit, "styled"][:, s * P : (s + 1) * P],
                    ident_f32[:],
                )
            epilogue[unit, "turned"] = turned

        def store(unit):
            first = unit[1] * PIXELS // P
            tiles = unit[2] * PIXELS // P
            result = result_pool.tile([P, tiles, FILTERS], F32, name="result")
            nc.scalar.copy(out=result[:], in_=epilogue[unit, "turned"][:])
            nc.sync.dma_start(out=out_rows[unit[0], :, first : first + tiles, :], in_=result[:])

        VECTOR_PLACES = {
            (1, 1): add_noise,
            (1, 2): leaky_relu,
            (2, 0): total,
            (2, 1): centre,
            (3, 0): variance,
            (3, 2): gain,
            (4, 0): scale_up,
            (4, 1): add_beta,
        }
        SCALAR_PLACES = {(2, 1): square, (3, 0): inverse, (5, 0): store}
        TENSOR_PLACES = {(4, 0): turn_back}

        def at(places, step, place):
            for (after, where), part in places.items():
                for group in range(GROUPS):
                    last_pass = mx_step(group * CHUNKS + CHUNKS - 1)
                    late = 1 if group == GROUPS - 2 and after > 2 else 0
                    if where == place and last_pass + after + late == step:
                        for unit in units(group):
                            part(unit)

        def scalar_epilogue(step, place):
            at(SCALAR_PLACES, step, place)

        def vector_epilogue(step, place):
            at(VECTOR_PLACES, step, place)

        for step in range(STEPS + 8):
            vector_epilogue(step, 0)
            sort_words(step, 0)
            vector_epilogue(step, 1)
            quantise(step - 1)
            if step == 8:
                copy_latents()
            if step == 9:
                copy_style()
            if step in W_STEPS:
                group_w(W_STEPS.index(step))
                quantise_w(W_STEPS.index(step))
            if step < STEPS:
                transpose(step)
            else:
                for place in range(CHUNK_PASSES):
                    scalar_epilogue(step, place)
                    if place == 1:
                        vector_epilogue(step, 2)
            load(step + X_BUFS)
            for i in range(STEPS):
                if mx_step(i) == step:
                    multiply(i)
            if 2 <= step < 6:
                noise_table((step - 2) * 512)
            if step == 7:
                turn_latents()
            if step == 8:
                style_table()
            at(TENSOR_PLACES, step, 0)
